import numpy as np
import ml_dtypes


def mxq(x, axis, fmt="e4m3"):
    dtype, down = {"e4m3": (ml_dtypes.float8_e4m3fn, 7), "e5m2": (ml_dtypes.float8_e5m2, 14)}[fmt]
    v = np.moveaxis(np.asarray(x, np.float32).astype(ml_dtypes.bfloat16).astype(np.float64), axis, -1)
    blocks = v.reshape(v.shape[:-1] + (-1, 32))
    amax = np.abs(blocks).max(-1, keepdims=True)
    byte = np.maximum(np.where(amax > 0, np.frexp(amax)[1] - 1 + 127, 0) - down, 1)
    scale = np.exp2(byte - 127.0)
    codes = (blocks / scale).astype(np.float32).astype(dtype).astype(np.float64)
    return np.moveaxis((codes * scale).reshape(v.shape), -1, axis)


WIDE = False


def mx_kscale(k):
    if not WIDE:
        return np.ones(k)
    levels = np.array([10, -10, 5, -5, 0])
    a = np.random.permutation(np.resize(levels, k // 512 * 4)).reshape(k // 512, 4)
    idx = np.arange(k)
    return np.exp2(a[idx // 512, idx % 128 // 32])


BF16 = ml_dtypes.bfloat16


def bf(x):
    return np.asarray(x, np.float32).astype(BF16)


def f64(x):
    return np.asarray(x).astype(np.float64)


B, S, D, DR = 2, 512, 1024, 1024
G = 1.4 * (D / DR) ** 0.25 / np.sqrt(D)


def setup_inputs():
    s = mx_kscale(D)
    t = mx_kscale(DR)
    mask = (np.random.random((S, S)) < 0.5) & ~np.eye(S, dtype=bool)
    return {"q_lin": bf(np.random.standard_normal((B, S, D)) * s),
            "k_lin": bf(np.random.standard_normal((B, S, D)) * s),
            "rotation_params": bf(np.random.standard_normal((DR, D)) * G * t[:, None] / s),
            "entangle_params": bf(np.random.standard_normal((DR, D)) * G / t[:, None] / s),
            "mask": mask}


def reference(q_lin, k_lin, rotation_params, entangle_params, mask):
    q = mxq(f64(q_lin), 2, "e4m3") @ mxq(f64(rotation_params), 1, "e4m3").T
    k = mxq(f64(k_lin), 2, "e4m3") @ mxq(f64(entangle_params), 1, "e4m3").T
    scores = (mxq(q, 2, "e4m3") @ mxq(k, 2, "e4m3").transpose(0, 2, 1)) / np.sqrt(D)
    scores = np.where(f64(mask) > 0.5, -np.inf, scores)
    e = np.exp(scores - scores.max(-1, keepdims=True))
    return e / e.sum(-1, keepdims=True)

@@ -1,0 +1,219 @@
+from contextlib import ExitStack
+
+import concourse.mybir as mybir
+from concourse.masks import make_identity
+
+F32 = mybir.dt.float32
+BF16 = mybir.dt.bfloat16
+I32 = mybir.dt.int32
+U32 = mybir.dt.uint32
+U8 = mybir.dt.uint8
+FP8X4 = mybir.dt.float8_e4m3fn_x4
+ALU = mybir.AluOpType
+ACT = mybir.ActivationFunctionType
+AXIS = mybir.AxisListType
+
+B, S, D, DR = 2, 512, 1024, 1024
+P = 128
+PACK = 4
+K_PASS = P * PACK
+BANK = 512
+D_PASSES = D // K_PASS
+DR_PASSES = DR // K_PASS
+TILES = 4
+ROW_WORDS = D // 2
+FAR = 1.5e38
+
+FLOPS = 2 * (2 * B * S * D * DR) + 2 * B * S * S * DR
+
+
+def tile_selfattention_pa_kernel(tc, q_lin, k_lin, rotation_params, entangle_params, mask, out):
+    nc = tc.nc
+    with ExitStack() as ctx:
+        keep = ctx.enter_context(tc.tile_pool(name="keep", bufs=1))
+        stage = ctx.enter_context(tc.tile_pool(name="stage", bufs=2))
+        soft = ctx.enter_context(tc.tile_pool(name="soft", bufs=3))
+        small = ctx.enter_context(tc.tile_pool(name="small", bufs=4))
+        psum = ctx.enter_context(tc.psum_pool(name="psum", bufs=8))
+        ctx.enter_context(tc.manual_schedule())
+
+        def load_chunk(name, rows_of_partition):
+            chunk = keep.tile([P, TILES * D], BF16, name=name)
+            nc.sync.dma_start(out=chunk[:].rearrange("p (i d) -> p i d", i=TILES), in_=rows_of_partition)
+            return chunk
+
+        def weight_rows(w, h):
+            return w.rearrange("(h p i) d -> h p i d", h=DR_PASSES, i=TILES)[h]
+
+        def token_rows(x, b):
+            return x[b].rearrange("(i p) d -> p i d", p=P)
+
+        ent_rows = [None] * DR_PASSES
+        rot_rows = [None] * DR_PASSES
+        k_rows = [None] * B
+        q_rows = [None] * B
+        ent_rows[0] = load_chunk("ent_rows0", weight_rows(entangle_params, 0))
+        k_rows[0] = load_chunk("k_rows0", token_rows(k_lin, 0))
+        ent_rows[1] = load_chunk("ent_rows1", weight_rows(entangle_params, 1))
+        rot_rows[0] = load_chunk("rot_rows0", weight_rows(rotation_params, 0))
+        rot_rows[1] = load_chunk("rot_rows1", weight_rows(rotation_params, 1))
+        q_rows[0] = load_chunk("q_rows0", token_rows(q_lin, 0))
+        k_rows[1] = load_chunk("k_rows1", token_rows(k_lin, 1))
+        mask_words = keep.tile([P, TILES, 2 * S], I32, name="mask_words")
+        for j in range(TILES):
+            nc.sync.dma_start(out=mask_words[:, j, :], in_=mask.bitcast(I32)[j * P : (j + 1) * P, :])
+        q_rows[1] = load_chunk("q_rows1", token_rows(q_lin, 1))
+
+        ident = keep.tile([P, P], F32, name="ident")
+        make_identity(nc, ident[:])
+
+        zero = small.tile([P, 1], F32, name="zero")
+        one = small.tile([P, 1], F32, name="one")
+        nc.vector.memset(zero[:], 0.0)
+        nc.scalar.activation(out=one[:], in_=zero[:], func=ACT.Exp)
+
+        def new_operand(name, shape):
+            codes = keep.tile([P] + shape, U32, name=name + "_codes", align_bytes=64)
+            scales = keep.tile([P] + shape, U8, name=name + "_scales", align_bytes=64)
+            return codes, scales
+
+        ent = [new_operand("ent%d" % h, [TILES, D_PASSES, P]) for h in range(DR_PASSES)]
+        rot = [new_operand("rot%d" % h, [TILES, D_PASSES, P]) for h in range(DR_PASSES)]
+        k_tok = [new_operand("k_tok%d" % b, [TILES, D_PASSES, P]) for b in range(B)]
+        q_tok = [new_operand("q_tok%d" % b, [TILES, D_PASSES, P]) for b in range(B)]
+        k_codes, k_scales = new_operand("k", [B, DR_PASSES, S])
+        q_codes, q_scales = new_operand("q", [B, TILES, DR_PASSES, P])
+
+        def empty_bank(n):
+            return nc.vector.tensor_copy if n == 1 else nc.scalar.copy
+
+        def quantise_chunk(chunk, operand):
+            codes, scales = operand
+            words = chunk[:].bitcast(F32)
+            grouped = stage.tile([P, TILES * D], BF16, tag="grouped", align_bytes=64)
+            grouped_words = grouped[:].bitcast(F32)
+            for i in range(TILES):
+                bank = psum.tile([P, BANK], F32, tag="bank")
+                for c in range(ROW_WORDS // P):
+                    column = i * ROW_WORDS + c * P
+                    nc.tensor.transpose(bank[:, c * P : (c + 1) * P], words[:, column : column + P], ident[:])
+                empty_bank(i)(
+                    out=grouped_words[:, i * ROW_WORDS : (i + 1) * ROW_WORDS].rearrange(
+                        "p (g r u) -> p g r u", g=D_PASSES, u=2
+                    ),
+                    in_=bank[:].rearrange("p (g u r) -> p g r u", g=D_PASSES, u=2),
+                )
+            nc.vector.quantize_mx(
+                out=codes[:].rearrange("p i g r -> p (i g r)").bitcast(FP8X4),
+                scales=scales[:].rearrange("p i g r -> p (i g r)"),
+                in_=grouped[:],
+            )
+
+        def project(weight, tokens, j, copy, grouped):
+            w_codes, w_scales = weight
+            x_codes, x_scales = tokens
+            bank = psum.tile([P, BANK], F32, tag="bank")
+            for t in range(PACK):
+                for g in range(D_PASSES):
+                    nc.tensor.matmul_mx(
+                        out=bank[:, t * P : (t + 1) * P],
+                        lhsT=w_codes[:, t, g, :].bitcast(FP8X4),
+                        lhsT_scale=w_scales[:, t, g, :],
+                        rhs=x_codes[:, j, g, :].bitcast(FP8X4),
+                        rhs_scale=x_scales[:, j, g, :],
+                        start=(g == 0),
+                        stop=(g == D_PASSES - 1),
+                    )
+            copy(
+                out=grouped.rearrange("p (r t) -> p r t", t=PACK),
+                in_=bank[:].rearrange("p (t r) -> p r t", t=PACK),
+            )
+
+        def project_keys(b, h):
+            grouped = stage.tile([P, TILES * BANK], BF16, tag="grouped_k", align_bytes=64)
+            for j in range(TILES):
+                project(ent[h], k_tok[b], j, empty_bank(j), grouped[:, j * BANK : (j + 1) * BANK])
+            nc.vector.quantize_mx(
+                out=k_codes[:, b, h, :].bitcast(FP8X4), scales=k_scales[:, b, h, :], in_=grouped[:]
+            )
+
+        def project_queries(b, j):
+            grouped = stage.tile([P, DR_PASSES * BANK], BF16, tag="grouped_q", align_bytes=64)
+            for h in range(DR_PASSES):
+                project(rot[h], q_tok[b], j, nc.scalar.copy, grouped[:, h * BANK : (h + 1) * BANK])
+            nc.vector.quantize_mx(
+                out=q_codes[:, b, j, :, :].rearrange("p h r -> p (h r)").bitcast(FP8X4),
+                scales=q_scales[:, b, j, :, :].rearrange("p h r -> p (h r)"),
+                in_=grouped[:],
+            )
+
+        bound = keep.tile([P, TILES, S], F32, name="bound")
+
+        def make_bound(j):
+            nc.vector.tensor_scalar(
+                out=bound[:, j, :],
+                in0=mask_words[:, j, 0 : 2 * S : 2],
+                scalar1=-2.0 * FAR,
+                scalar2=FAR,
+                op0=ALU.mult,
+                op1=ALU.add,
+            )
+
+        def scores_and_max(b, j):
+            bank = psum.tile([P, BANK], F32, tag="bank")
+            for h in range(DR_PASSES):
+                nc.tensor.matmul_mx(
+                    out=bank[:],
+                    lhsT=q_codes[:, b, j, h, :].bitcast(FP8X4),
+                    lhsT_scale=q_scales[:, b, j, h, :],
+                    rhs=k_codes[:, b, h, :].bitcast(FP8X4),
+                    rhs_scale=k_scales[:, b, h, :],
+                    start=(h == 0),
+                    stop=(h == DR_PASSES - 1),
+                )
+            if b == 0:
+                make_bound(j)
+            masked = soft.tile([P, S], F32, tag="masked")
+            nc.vector.scalar_tensor_tensor(
+                out=masked[:], in0=bank[:], scalar=D**-0.5, in1=bound[:, j, :], op0=ALU.mult, op1=ALU.min
+            )
+            neg_max = small.tile([P, 1], F32, tag="neg_max")
+            nc.vector.tensor_reduce(out=neg_max[:], in_=masked[:], axis=AXIS.X, op=ALU.max, negate=True)
+            return masked, neg_max
+
+        def exp_normalise_store(b, j, masked, neg_max):
+            expd = soft.tile([P, S], F32, tag="expd")
+            row_sum = small.tile([P, 1], F32, tag="row_sum")
+            nc.scalar.activation(
+                out=expd[:], in_=masked[:], func=ACT.Exp, bias=neg_max[:], scale=1.0, accum_out=row_sum[:]
+            )
+            inverse = small.tile([P, 1], F32, tag="inverse")
+            nc.vector.reciprocal(out=inverse[:], in_=row_sum[:])
+            weights = soft.tile([P, S], F32, tag="weights")
+            nc.vector.tensor_scalar_mul(out=weights[:], in0=expd[:], scalar1=inverse[:])
+            nc.sync.dma_start(out=out[b, j * P : (j + 1) * P, :], in_=weights[:])
+
+        quantise_chunk(ent_rows[0], ent[0])
+        quantise_chunk(k_rows[0], k_tok[0])
+        quantise_chunk(ent_rows[1], ent[1])
+        project_keys(0, 0)
+        quantise_chunk(rot_rows[0], rot[0])
+        project_keys(0, 1)
+        quantise_chunk(rot_rows[1], rot[1])
+        quantise_chunk(q_rows[0], q_tok[0])
+        quantise_chunk(k_rows[1], k_tok[1])
+
+        for b in range(B):
+            waiting = [None] * TILES
+            for step in range(TILES + 2):
+                if b == 0 and step == TILES:
+                    project_keys(1, 0)
+                if b == 0 and step == TILES + 1:
+                    quantise_chunk(q_rows[1], q_tok[1])
+                    project_keys(1, 1)
+                if step < TILES:
+                    project_queries(b, step)
+                if 1 <= step <= TILES:
+                    waiting[step - 1] = scores_and_max(b, step - 1)
+                if step >= 2:
+                    exp_normalise_store(b, step - 2, *waiting[step - 2])

@@ -35,7 +35,6 @@ def tile_selfattention_pa_kernel(tc, q_lin, k_lin, rotation_params, entangle_par
         soft = ctx.enter_context(tc.tile_pool(name="soft", bufs=3))
         small = ctx.enter_context(tc.tile_pool(name="small", bufs=4))
         psum = ctx.enter_context(tc.psum_pool(name="psum", bufs=8))
-        ctx.enter_context(tc.manual_schedule())
 
         def load_chunk(name, rows_of_partition):
             chunk = keep.tile([P, TILES * D], BF16, name=name)

@@ -22,6 +22,8 @@ D_PASSES = D // K_PASS
 DR_PASSES = DR // K_PASS
 TILES = 4
 ROW_WORDS = D // 2
+QUERY_TILES = B * TILES
+AHEAD = 2
 FAR = 1.5e38
 
 FLOPS = 2 * (2 * B * S * D * DR) + 2 * B * S * S * DR
@@ -31,14 +33,16 @@ def tile_selfattention_pa_kernel(tc, q_lin, k_lin, rotation_params, entangle_par
     nc = tc.nc
     with ExitStack() as ctx:
         keep = ctx.enter_context(tc.tile_pool(name="keep", bufs=1))
-        stage = ctx.enter_context(tc.tile_pool(name="stage", bufs=2))
+        stage = ctx.enter_context(tc.tile_pool(name="stage", bufs=3))
         soft = ctx.enter_context(tc.tile_pool(name="soft", bufs=3))
         small = ctx.enter_context(tc.tile_pool(name="small", bufs=4))
         psum = ctx.enter_context(tc.psum_pool(name="psum", bufs=8))
+        ctx.enter_context(tc.manual_schedule())
 
         def load_chunk(name, rows_of_partition):
             chunk = keep.tile([P, TILES * D], BF16, name=name)
-            nc.sync.dma_start(out=chunk[:].rearrange("p (i d) -> p i d", i=TILES), in_=rows_of_partition)
+            for i in range(TILES):
+                nc.sync.dma_start(out=chunk[:, i * D : (i + 1) * D], in_=rows_of_partition[:, i, :])
             return chunk
 
         def weight_rows(w, h):
@@ -58,10 +62,10 @@ def tile_selfattention_pa_kernel(tc, q_lin, k_lin, rotation_params, entangle_par
         rot_rows[1] = load_chunk("rot_rows1", weight_rows(rotation_params, 1))
         q_rows[0] = load_chunk("q_rows0", token_rows(q_lin, 0))
         k_rows[1] = load_chunk("k_rows1", token_rows(k_lin, 1))
+        q_rows[1] = load_chunk("q_rows1", token_rows(q_lin, 1))
         mask_words = keep.tile([P, TILES, 2 * S], I32, name="mask_words")
         for j in range(TILES):
             nc.sync.dma_start(out=mask_words[:, j, :], in_=mask.bitcast(I32)[j * P : (j + 1) * P, :])
-        q_rows[1] = load_chunk("q_rows1", token_rows(q_lin, 1))
 
         ident = keep.tile([P, P], F32, name="ident")
         make_identity(nc, ident[:])
@@ -80,23 +84,21 @@ def tile_selfattention_pa_kernel(tc, q_lin, k_lin, rotation_params, entangle_par
         rot = [new_operand("rot%d" % h, [TILES, D_PASSES, P]) for h in range(DR_PASSES)]
         k_tok = [new_operand("k_tok%d" % b, [TILES, D_PASSES, P]) for b in range(B)]
         q_tok = [new_operand("q_tok%d" % b, [TILES, D_PASSES, P]) for b in range(B)]
-        k_codes, k_scales = new_operand("k", [B, DR_PASSES, S])
-        q_codes, q_scales = new_operand("q", [B, TILES, DR_PASSES, P])
-
-        def empty_bank(n):
-            return nc.vector.tensor_copy if n == 1 else nc.scalar.copy
+        k_mx = new_operand("k", [B, DR_PASSES, S])
+        q_mx = new_operand("q", [B, DR_PASSES, S])
 
         def quantise_chunk(chunk, operand):
             codes, scales = operand
             words = chunk[:].bitcast(F32)
-            grouped = stage.tile([P, TILES * D], BF16, tag="grouped", align_bytes=64)
+            grouped = stage.tile([P, TILES * D], BF16, tag="grouped_rows", align_bytes=64)
             grouped_words = grouped[:].bitcast(F32)
             for i in range(TILES):
                 bank = psum.tile([P, BANK], F32, tag="bank")
                 for c in range(ROW_WORDS // P):
                     column = i * ROW_WORDS + c * P
                     nc.tensor.transpose(bank[:, c * P : (c + 1) * P], words[:, column : column + P], ident[:])
-                empty_bank(i)(
+                copy = nc.vector.tensor_copy if i == 1 else nc.scalar.copy
+                copy(
                     out=grouped_words[:, i * ROW_WORDS : (i + 1) * ROW_WORDS].rearrange(
                         "p (g r u) -> p g r u", g=D_PASSES, u=2
                     ),
@@ -108,111 +110,136 @@ def tile_selfattention_pa_kernel(tc, q_lin, k_lin, rotation_params, entangle_par
                 in_=grouped[:],
             )
 
-        def project(weight, tokens, j, copy, grouped):
-            w_codes, w_scales = weight
-            x_codes, x_scales = tokens
-            bank = psum.tile([P, BANK], F32, tag="bank")
-            for t in range(PACK):
-                for g in range(D_PASSES):
-                    nc.tensor.matmul_mx(
-                        out=bank[:, t * P : (t + 1) * P],
-                        lhsT=w_codes[:, t, g, :].bitcast(FP8X4),
-                        lhsT_scale=w_scales[:, t, g, :],
-                        rhs=x_codes[:, j, g, :].bitcast(FP8X4),
-                        rhs_scale=x_scales[:, j, g, :],
-                        start=(g == 0),
-                        stop=(g == D_PASSES - 1),
-                    )
-            copy(
-                out=grouped.rearrange("p (r t) -> p r t", t=PACK),
-                in_=bank[:].rearrange("p (t r) -> p r t", t=PACK),
-            )
-
-        def project_keys(b, h):
-            grouped = stage.tile([P, TILES * BANK], BF16, tag="grouped_k", align_bytes=64)
-            for j in range(TILES):
-                project(ent[h], k_tok[b], j, empty_bank(j), grouped[:, j * BANK : (j + 1) * BANK])
+        def project(weight, tokens, projected, b, h, first, count):
+            w_codes, w_scales = weight[h]
+            x_codes, x_scales = tokens[b]
+            codes, scales = projected
+            grouped = stage.tile([P, 2 * BANK], BF16, tag="grouped_tokens", align_bytes=64)
+            for n in range(count):
+                bank = psum.tile([P, BANK], F32, tag="bank")
+                for t in range(PACK):
+                    for g in range(D_PASSES):
+                        nc.tensor.matmul_mx(
+                            out=bank[:, t * P : (t + 1) * P],
+                            lhsT=w_codes[:, t, g, :].bitcast(FP8X4),
+                            lhsT_scale=w_scales[:, t, g, :],
+                            rhs=x_codes[:, first + n, g, :].bitcast(FP8X4),
+                            rhs_scale=x_scales[:, first + n, g, :],
+                            start=(g == 0),
+                            stop=(g == D_PASSES - 1),
+                        )
+                nc.scalar.copy(
+                    out=grouped[:, n * BANK : (n + 1) * BANK].rearrange("p (r t) -> p r t", t=PACK),
+                    in_=bank[:].rearrange("p (t r) -> p r t", t=PACK),
+                )
             nc.vector.quantize_mx(
-                out=k_codes[:, b, h, :].bitcast(FP8X4), scales=k_scales[:, b, h, :], in_=grouped[:]
+                out=codes[:, b, h, first * P : (first + count) * P].bitcast(FP8X4),
+                scales=scales[:, b, h, first * P : (first + count) * P],
+                in_=grouped[:, 0 : count * BANK],
             )
 
-        def project_queries(b, j):
-            grouped = stage.tile([P, DR_PASSES * BANK], BF16, tag="grouped_q", align_bytes=64)
+        def project_keys(b, h, first, count):
+            project(ent, k_tok, k_mx, b, h, first, count)
+
+        def project_query_tile(n):
             for h in range(DR_PASSES):
-                project(rot[h], q_tok[b], j, nc.scalar.copy, grouped[:, h * BANK : (h + 1) * BANK])
-            nc.vector.quantize_mx(
-                out=q_codes[:, b, j, :, :].rearrange("p h r -> p (h r)").bitcast(FP8X4),
-                scales=q_scales[:, b, j, :, :].rearrange("p h r -> p (h r)"),
-                in_=grouped[:],
-            )
+                project(rot, q_tok, q_mx, n // TILES, h, n % TILES, 1)
 
-        bound = keep.tile([P, TILES, S], F32, name="bound")
+        masked = [None] * QUERY_TILES
+        neg_max = [None] * QUERY_TILES
+        bias = [None] * QUERY_TILES
+        expd = [None] * QUERY_TILES
+        row_sum = [None] * QUERY_TILES
+        inverse = [None] * QUERY_TILES
 
-        def make_bound(j):
-            nc.vector.tensor_scalar(
-                out=bound[:, j, :],
-                in0=mask_words[:, j, 0 : 2 * S : 2],
-                scalar1=-2.0 * FAR,
-                scalar2=FAR,
-                op0=ALU.mult,
-                op1=ALU.add,
-            )
-
-        def scores_and_max(b, j):
+        def scores(n):
+            b, j = n // TILES, n % TILES
+            q_codes, q_scales = q_mx
+            k_codes, k_scales = k_mx
             bank = psum.tile([P, BANK], F32, tag="bank")
             for h in range(DR_PASSES):
                 nc.tensor.matmul_mx(
                     out=bank[:],
-                    lhsT=q_codes[:, b, j, h, :].bitcast(FP8X4),
-                    lhsT_scale=q_scales[:, b, j, h, :],
+                    lhsT=q_codes[:, b, h, j * P : (j + 1) * P].bitcast(FP8X4),
+                    lhsT_scale=q_scales[:, b, h, j * P : (j + 1) * P],
                     rhs=k_codes[:, b, h, :].bitcast(FP8X4),
                     rhs_scale=k_scales[:, b, h, :],
                     start=(h == 0),
                     stop=(h == DR_PASSES - 1),
                 )
-            if b == 0:
-                make_bound(j)
-            masked = soft.tile([P, S], F32, tag="masked")
-            nc.vector.scalar_tensor_tensor(
-                out=masked[:], in0=bank[:], scalar=D**-0.5, in1=bound[:, j, :], op0=ALU.mult, op1=ALU.min
-            )
-            neg_max = small.tile([P, 1], F32, tag="neg_max")
-            nc.vector.tensor_reduce(out=neg_max[:], in_=masked[:], axis=AXIS.X, op=ALU.max, negate=True)
-            return masked, neg_max
+            return bank
 
-        def exp_normalise_store(b, j, masked, neg_max):
-            expd = soft.tile([P, S], F32, tag="expd")
-            row_sum = small.tile([P, 1], F32, tag="row_sum")
-            nc.scalar.activation(
-                out=expd[:], in_=masked[:], func=ACT.Exp, bias=neg_max[:], scale=1.0, accum_out=row_sum[:]
+        def mask_scores(n, bank):
+            masked[n] = soft.tile([P, S], F32, name="masked%d" % n, tag="masked")
+            nc.vector.scalar_tensor_tensor(
+                out=masked[n][:],
+                in0=mask_words[:, n % TILES, 0 : 2 * S : 2],
+                scalar=-FAR,
+                in1=bank[:],
+                op0=ALU.mult,
+                op1=ALU.add,
             )
-            inverse = small.tile([P, 1], F32, tag="inverse")
-            nc.vector.reciprocal(out=inverse[:], in_=row_sum[:])
+
+        def row_maximum(n):
+            neg_max[n] = small.tile([P, 1], F32, name="neg_max%d" % n, tag="neg_max")
+            nc.vector.tensor_reduce(out=neg_max[n][:], in_=masked[n][:], axis=AXIS.X, op=ALU.max, negate=True)
+
+        def exponent_bias(n):
+            bias[n] = small.tile([P, 1], F32, name="bias%d" % n, tag="bias")
+            nc.vector.tensor_scalar_mul(out=bias[n][:], in0=neg_max[n][:], scalar1=D**-0.5)
+
+        def exponentials(n):
+            expd[n] = soft.tile([P, S], F32, name="expd%d" % n, tag="expd")
+            row_sum[n] = small.tile([P, 1], F32, name="row_sum%d" % n, tag="row_sum")
+            nc.scalar.activation(
+                out=expd[n][:],
+                in_=masked[n][:],
+                func=ACT.Exp,
+                bias=bias[n][:],
+                scale=D**-0.5,
+                accum_out=row_sum[n][:],
+            )
+
+        def invert_row_sum(n):
+            inverse[n] = small.tile([P, 1], F32, name="inverse%d" % n, tag="inverse")
+            nc.vector.reciprocal(out=inverse[n][:], in_=row_sum[n][:])
+
+        def normalise_and_store(n):
             weights = soft.tile([P, S], F32, tag="weights")
-            nc.vector.tensor_scalar_mul(out=weights[:], in0=expd[:], scalar1=inverse[:])
-            nc.sync.dma_start(out=out[b, j * P : (j + 1) * P, :], in_=weights[:])
+            nc.vector.tensor_scalar_mul(out=weights[:], in0=expd[n][:], scalar1=inverse[n][:])
+            nc.sync.dma_start(out=out[n // TILES, (n % TILES) * P : (n % TILES + 1) * P, :], in_=weights[:])
 
         quantise_chunk(ent_rows[0], ent[0])
         quantise_chunk(k_rows[0], k_tok[0])
         quantise_chunk(ent_rows[1], ent[1])
-        project_keys(0, 0)
+        project_keys(0, 0, 0, 2)
         quantise_chunk(rot_rows[0], rot[0])
-        project_keys(0, 1)
+        project_keys(0, 0, 2, 2)
         quantise_chunk(rot_rows[1], rot[1])
+        project_keys(0, 1, 0, 2)
         quantise_chunk(q_rows[0], q_tok[0])
+        project_keys(0, 1, 2, 2)
         quantise_chunk(k_rows[1], k_tok[1])
+        for n in range(AHEAD):
+            project_query_tile(n)
+        quantise_chunk(q_rows[1], q_tok[1])
 
-        for b in range(B):
-            waiting = [None] * TILES
-            for step in range(TILES + 2):
-                if b == 0 and step == TILES:
-                    project_keys(1, 0)
-                if b == 0 and step == TILES + 1:
-                    quantise_chunk(q_rows[1], q_tok[1])
-                    project_keys(1, 1)
-                if step < TILES:
-                    project_queries(b, step)
-                if 1 <= step <= TILES:
-                    waiting[step - 1] = scores_and_max(b, step - 1)
-                if step >= 2:
-                    exp_normalise_store(b, step - 2, *waiting[step - 2])
+        for n in range(QUERY_TILES + 1):
+            if n < QUERY_TILES:
+                bank = scores(n)
+            if n >= 1:
+                exponentials(n - 1)
+            if n < QUERY_TILES:
+                mask_scores(n, bank)
+            if n >= 1:
+                invert_row_sum(n - 1)
+            if n < QUERY_TILES:
+                row_maximum(n)
+            if n >= 1:
+                normalise_and_store(n - 1)
+            if n < QUERY_TILES:
+                exponent_bias(n)
+            if n < TILES:
+                project_keys(1, n // 2, 2 * (n % 2), 2)
+            if n + AHEAD < QUERY_TILES:
+                project_query_tile(n + AHEAD)

@@ -25,6 +25,8 @@ ROW_WORDS = D // 2
 QUERY_TILES = B * TILES
 AHEAD = 2
 FAR = 1.5e38
+SCORE_SCALE = D**-0.5
+assert SCORE_SCALE == 2.0**-5
 
 FLOPS = 2 * (2 * B * S * D * DR) + 2 * B * S * S * DR
 
@@ -110,7 +112,7 @@ def tile_selfattention_pa_kernel(tc, q_lin, k_lin, rotation_params, entangle_par
                 in_=grouped[:],
             )
 
-        def project(weight, tokens, projected, b, h, first, count):
+        def project(weight, tokens, projected, leave_psum, b, h, first, count):
             w_codes, w_scales = weight[h]
             x_codes, x_scales = tokens[b]
             codes, scales = projected
@@ -128,7 +130,7 @@ def tile_selfattention_pa_kernel(tc, q_lin, k_lin, rotation_params, entangle_par
                             start=(g == 0),
                             stop=(g == D_PASSES - 1),
                         )
-                nc.scalar.copy(
+                leave_psum(
                     out=grouped[:, n * BANK : (n + 1) * BANK].rearrange("p (r t) -> p r t", t=PACK),
                     in_=bank[:].rearrange("p (t r) -> p r t", t=PACK),
                 )
@@ -139,15 +141,17 @@ def tile_selfattention_pa_kernel(tc, q_lin, k_lin, rotation_params, entangle_par
             )
 
         def project_keys(b, h, first, count):
-            project(ent, k_tok, k_mx, b, h, first, count)
+            project(ent, k_tok, k_mx, nc.scalar.copy, b, h, first, count)
+
+        def copy_scaled(out, in_):
+            nc.scalar.mul(out=out, in_=in_, mul=SCORE_SCALE)
 
         def project_query_tile(n):
             for h in range(DR_PASSES):
-                project(rot, q_tok, q_mx, n // TILES, h, n % TILES, 1)
+                project(rot, q_tok, q_mx, copy_scaled, n // TILES, h, n % TILES, 1)
 
         masked = [None] * QUERY_TILES
         neg_max = [None] * QUERY_TILES
-        bias = [None] * QUERY_TILES
         expd = [None] * QUERY_TILES
         row_sum = [None] * QUERY_TILES
         inverse = [None] * QUERY_TILES
@@ -184,10 +188,6 @@ def tile_selfattention_pa_kernel(tc, q_lin, k_lin, rotation_params, entangle_par
             neg_max[n] = small.tile([P, 1], F32, name="neg_max%d" % n, tag="neg_max")
             nc.vector.tensor_reduce(out=neg_max[n][:], in_=masked[n][:], axis=AXIS.X, op=ALU.max, negate=True)
 
-        def exponent_bias(n):
-            bias[n] = small.tile([P, 1], F32, name="bias%d" % n, tag="bias")
-            nc.vector.tensor_scalar_mul(out=bias[n][:], in0=neg_max[n][:], scalar1=D**-0.5)
-
         def exponentials(n):
             expd[n] = soft.tile([P, S], F32, name="expd%d" % n, tag="expd")
             row_sum[n] = small.tile([P, 1], F32, name="row_sum%d" % n, tag="row_sum")
@@ -195,8 +195,8 @@ def tile_selfattention_pa_kernel(tc, q_lin, k_lin, rotation_params, entangle_par
                 out=expd[n][:],
                 in_=masked[n][:],
                 func=ACT.Exp,
-                bias=bias[n][:],
-                scale=D**-0.5,
+                bias=neg_max[n][:],
+                scale=1.0,
                 accum_out=row_sum[n][:],
             )
 
@@ -237,8 +237,6 @@ def tile_selfattention_pa_kernel(tc, q_lin, k_lin, rotation_params, entangle_par
                 row_maximum(n)
             if n >= 1:
                 normalise_and_store(n - 1)
-            if n < QUERY_TILES:
-                exponent_bias(n)
             if n < TILES:
                 project_keys(1, n // 2, 2 * (n % 2), 2)
             if n + AHEAD < QUERY_TILES:

@@ -23,7 +23,7 @@ DR_PASSES = DR // K_PASS
 TILES = 4
 ROW_WORDS = D // 2
 QUERY_TILES = B * TILES
-AHEAD = 2
+AHEAD = 3
 FAR = 1.5e38
 SCORE_SCALE = D**-0.5
 assert SCORE_SCALE == 2.0**-5

from contextlib import ExitStack

import concourse.mybir as mybir
from concourse.masks import make_identity

F32 = mybir.dt.float32
BF16 = mybir.dt.bfloat16
I32 = mybir.dt.int32
U32 = mybir.dt.uint32
U8 = mybir.dt.uint8
FP8X4 = mybir.dt.float8_e4m3fn_x4
ALU = mybir.AluOpType
ACT = mybir.ActivationFunctionType
AXIS = mybir.AxisListType

B, S, D, DR = 2, 512, 1024, 1024
P = 128
PACK = 4
K_PASS = P * PACK
BANK = 512
D_PASSES = D // K_PASS
DR_PASSES = DR // K_PASS
TILES = 4
ROW_WORDS = D // 2
QUERY_TILES = B * TILES
AHEAD = 3
FAR = 1.5e38
SCORE_SCALE = D**-0.5
assert SCORE_SCALE == 2.0**-5

FLOPS = 2 * (2 * B * S * D * DR) + 2 * B * S * S * DR


def tile_selfattention_pa_kernel(tc, q_lin, k_lin, rotation_params, entangle_params, mask, out):
    nc = tc.nc
    with ExitStack() as ctx:
        keep = ctx.enter_context(tc.tile_pool(name="keep", bufs=1))
        stage = ctx.enter_context(tc.tile_pool(name="stage", bufs=3))
        soft = ctx.enter_context(tc.tile_pool(name="soft", bufs=3))
        small = ctx.enter_context(tc.tile_pool(name="small", bufs=4))
        psum = ctx.enter_context(tc.psum_pool(name="psum", bufs=8))
        ctx.enter_context(tc.manual_schedule())

        def load_chunk(name, rows_of_partition):
            chunk = keep.tile([P, TILES * D], BF16, name=name)
            for i in range(TILES):
                nc.sync.dma_start(out=chunk[:, i * D : (i + 1) * D], in_=rows_of_partition[:, i, :])
            return chunk

        def weight_rows(w, h):
            return w.rearrange("(h p i) d -> h p i d", h=DR_PASSES, i=TILES)[h]

        def token_rows(x, b):
            return x[b].rearrange("(i p) d -> p i d", p=P)

        ent_rows = [None] * DR_PASSES
        rot_rows = [None] * DR_PASSES
        k_rows = [None] * B
        q_rows = [None] * B
        ent_rows[0] = load_chunk("ent_rows0", weight_rows(entangle_params, 0))
        k_rows[0] = load_chunk("k_rows0", token_rows(k_lin, 0))
        ent_rows[1] = load_chunk("ent_rows1", weight_rows(entangle_params, 1))
        rot_rows[0] = load_chunk("rot_rows0", weight_rows(rotation_params, 0))
        rot_rows[1] = load_chunk("rot_rows1", weight_rows(rotation_params, 1))
        q_rows[0] = load_chunk("q_rows0", token_rows(q_lin, 0))
        k_rows[1] = load_chunk("k_rows1", token_rows(k_lin, 1))
        q_rows[1] = load_chunk("q_rows1", token_rows(q_lin, 1))
        mask_words = keep.tile([P, TILES, 2 * S], I32, name="mask_words")
        for j in range(TILES):
            nc.sync.dma_start(out=mask_words[:, j, :], in_=mask.bitcast(I32)[j * P : (j + 1) * P, :])

        ident = keep.tile([P, P], F32, name="ident")
        make_identity(nc, ident[:])

        zero = small.tile([P, 1], F32, name="zero")
        one = small.tile([P, 1], F32, name="one")
        nc.vector.memset(zero[:], 0.0)
        nc.scalar.activation(out=one[:], in_=zero[:], func=ACT.Exp)

        def new_operand(name, shape):
            codes = keep.tile([P] + shape, U32, name=name + "_codes", align_bytes=64)
            scales = keep.tile([P] + shape, U8, name=name + "_scales", align_bytes=64)
            return codes, scales

        ent = [new_operand("ent%d" % h, [TILES, D_PASSES, P]) for h in range(DR_PASSES)]
        rot = [new_operand("rot%d" % h, [TILES, D_PASSES, P]) for h in range(DR_PASSES)]
        k_tok = [new_operand("k_tok%d" % b, [TILES, D_PASSES, P]) for b in range(B)]
        q_tok = [new_operand("q_tok%d" % b, [TILES, D_PASSES, P]) for b in range(B)]
        k_mx = new_operand("k", [B, DR_PASSES, S])
        q_mx = new_operand("q", [B, DR_PASSES, S])

        def quantise_chunk(chunk, operand):
            codes, scales = operand
            words = chunk[:].bitcast(F32)
            grouped = stage.tile([P, TILES * D], BF16, tag="grouped_rows", align_bytes=64)
            grouped_words = grouped[:].bitcast(F32)
            for i in range(TILES):
                bank = psum.tile([P, BANK], F32, tag="bank")
                for c in range(ROW_WORDS // P):
                    column = i * ROW_WORDS + c * P
                    nc.tensor.transpose(bank[:, c * P : (c + 1) * P], words[:, column : column + P], ident[:])
                copy = nc.vector.tensor_copy if i == 1 else nc.scalar.copy
                copy(
                    out=grouped_words[:, i * ROW_WORDS : (i + 1) * ROW_WORDS].rearrange(
                        "p (g r u) -> p g r u", g=D_PASSES, u=2
                    ),
                    in_=bank[:].rearrange("p (g u r) -> p g r u", g=D_PASSES, u=2),
                )
            nc.vector.quantize_mx(
                out=codes[:].rearrange("p i g r -> p (i g r)").bitcast(FP8X4),
                scales=scales[:].rearrange("p i g r -> p (i g r)"),
                in_=grouped[:],
            )

        def project(weight, tokens, projected, leave_psum, b, h, first, count):
            w_codes, w_scales = weight[h]
            x_codes, x_scales = tokens[b]
            codes, scales = projected
            grouped = stage.tile([P, 2 * BANK], BF16, tag="grouped_tokens", align_bytes=64)
            for n in range(count):
                bank = psum.tile([P, BANK], F32, tag="bank")
                for t in range(PACK):
                    for g in range(D_PASSES):
                        nc.tensor.matmul_mx(
                            out=bank[:, t * P : (t + 1) * P],
                            lhsT=w_codes[:, t, g, :].bitcast(FP8X4),
                            lhsT_scale=w_scales[:, t, g, :],
                            rhs=x_codes[:, first + n, g, :].bitcast(FP8X4),
                            rhs_scale=x_scales[:, first + n, g, :],
                            start=(g == 0),
                            stop=(g == D_PASSES - 1),
                        )
                leave_psum(
                    out=grouped[:, n * BANK : (n + 1) * BANK].rearrange("p (r t) -> p r t", t=PACK),
                    in_=bank[:].rearrange("p (t r) -> p r t", t=PACK),
                )
            nc.vector.quantize_mx(
                out=codes[:, b, h, first * P : (first + count) * P].bitcast(FP8X4),
                scales=scales[:, b, h, first * P : (first + count) * P],
                in_=grouped[:, 0 : count * BANK],
            )

        def project_keys(b, h, first, count):
            project(ent, k_tok, k_mx, nc.scalar.copy, b, h, first, count)

        def copy_scaled(out, in_):
            nc.scalar.mul(out=out, in_=in_, mul=SCORE_SCALE)

        def project_query_tile(n):
            for h in range(DR_PASSES):
                project(rot, q_tok, q_mx, copy_scaled, n // TILES, h, n % TILES, 1)

        masked = [None] * QUERY_TILES
        neg_max = [None] * QUERY_TILES
        expd = [None] * QUERY_TILES
        row_sum = [None] * QUERY_TILES
        inverse = [None] * QUERY_TILES

        def scores(n):
            b, j = n // TILES, n % TILES
            q_codes, q_scales = q_mx
            k_codes, k_scales = k_mx
            bank = psum.tile([P, BANK], F32, tag="bank")
            for h in range(DR_PASSES):
                nc.tensor.matmul_mx(
                    out=bank[:],
                    lhsT=q_codes[:, b, h, j * P : (j + 1) * P].bitcast(FP8X4),
                    lhsT_scale=q_scales[:, b, h, j * P : (j + 1) * P],
                    rhs=k_codes[:, b, h, :].bitcast(FP8X4),
                    rhs_scale=k_scales[:, b, h, :],
                    start=(h == 0),
                    stop=(h == DR_PASSES - 1),
                )
            return bank

        def mask_scores(n, bank):
            masked[n] = soft.tile([P, S], F32, name="masked%d" % n, tag="masked")
            nc.vector.scalar_tensor_tensor(
                out=masked[n][:],
                in0=mask_words[:, n % TILES, 0 : 2 * S : 2],
                scalar=-FAR,
                in1=bank[:],
                op0=ALU.mult,
                op1=ALU.add,
            )

        def row_maximum(n):
            neg_max[n] = small.tile([P, 1], F32, name="neg_max%d" % n, tag="neg_max")
            nc.vector.tensor_reduce(out=neg_max[n][:], in_=masked[n][:], axis=AXIS.X, op=ALU.max, negate=True)

        def exponentials(n):
            expd[n] = soft.tile([P, S], F32, name="expd%d" % n, tag="expd")
            row_sum[n] = small.tile([P, 1], F32, name="row_sum%d" % n, tag="row_sum")
            nc.scalar.activation(
                out=expd[n][:],
                in_=masked[n][:],
                func=ACT.Exp,
                bias=neg_max[n][:],
                scale=1.0,
                accum_out=row_sum[n][:],
            )

        def invert_row_sum(n):
            inverse[n] = small.tile([P, 1], F32, name="inverse%d" % n, tag="inverse")
            nc.vector.reciprocal(out=inverse[n][:], in_=row_sum[n][:])

        def normalise_and_store(n):
            weights = soft.tile([P, S], F32, tag="weights")
            nc.vector.tensor_scalar_mul(out=weights[:], in0=expd[n][:], scalar1=inverse[n][:])
            nc.sync.dma_start(out=out[n // TILES, (n % TILES) * P : (n % TILES + 1) * P, :], in_=weights[:])

        quantise_chunk(ent_rows[0], ent[0])
        quantise_chunk(k_rows[0], k_tok[0])
        quantise_chunk(ent_rows[1], ent[1])
        project_keys(0, 0, 0, 2)
        quantise_chunk(rot_rows[0], rot[0])
        project_keys(0, 0, 2, 2)
        quantise_chunk(rot_rows[1], rot[1])
        project_keys(0, 1, 0, 2)
        quantise_chunk(q_rows[0], q_tok[0])
        project_keys(0, 1, 2, 2)
        quantise_chunk(k_rows[1], k_tok[1])
        for n in range(AHEAD):
            project_query_tile(n)
        quantise_chunk(q_rows[1], q_tok[1])

        for n in range(QUERY_TILES + 1):
            if n < QUERY_TILES:
                bank = scores(n)
            if n >= 1:
                exponentials(n - 1)
            if n < QUERY_TILES:
                mask_scores(n, bank)
            if n >= 1:
                invert_row_sum(n - 1)
            if n < QUERY_TILES:
                row_maximum(n)
            if n >= 1:
                normalise_and_store(n - 1)
            if n < TILES:
                project_keys(1, n // 2, 2 * (n % 2), 2)
            if n + AHEAD < QUERY_TILES:
                project_query_tile(n + AHEAD)
